import numpy as np
import ml_dtypes


def mxq(x, axis, fmt="e4m3"):
    dtype, down = {"e4m3": (ml_dtypes.float8_e4m3fn, 7), "e5m2": (ml_dtypes.float8_e5m2, 14)}[fmt]
    v = np.moveaxis(np.asarray(x, np.float32).astype(ml_dtypes.bfloat16).astype(np.float64), axis, -1)
    blocks = v.reshape(v.shape[:-1] + (-1, 32))
    amax = np.abs(blocks).max(-1, keepdims=True)
    byte = np.maximum(np.where(amax > 0, np.frexp(amax)[1] - 1 + 127, 0) - down, 1)
    scale = np.exp2(byte - 127.0)
    codes = (blocks / scale).astype(np.float32).astype(dtype).astype(np.float64)
    return np.moveaxis((codes * scale).reshape(v.shape), -1, axis)


WIDE = False


def mx_kscale(k):
    if not WIDE:
        return np.ones(k)
    levels = np.array([30, -30])
    if k % 512:
        return np.exp2(np.random.permutation(np.resize(levels, k // 32))).repeat(32)
    a = np.empty((k // 512, 16))
    for p in range(k // 512):
        a[p, :8] = np.random.permutation(np.resize(levels, 8))
        for g in range(8):
            far = levels[np.abs(levels - a[p, g]) >= 10]
            a[p, g + 8] = far[np.random.randint(len(far))]
    return np.exp2(a.ravel()).repeat(32)


BF16 = ml_dtypes.bfloat16


def bf(x):
    return np.asarray(x, np.float32).astype(BF16)


def f64(x):
    return np.asarray(x).astype(np.float64)


B, N, DIM, H, HKV, D, CACHE, WINDOW = 1, 512, 2048, 16, 4, 128, 1536, 1024
EPS = 1e-6
THETA = 10000.0
HALF = D // 2


def rms_norm(t, w):
    return t * (1.0 / np.sqrt(np.mean(t * t, axis=-1, keepdims=True) + EPS)) * w


def rope(t, cos, sin):
    t2 = t.reshape(*t.shape[:-1], HALF, 2)
    x0, x1 = t2[..., 0], t2[..., 1]
    c = cos[None, None, :, :]
    s = sin[None, None, :, :]
    r0 = x0 * c - x1 * s
    r1 = x0 * s + x1 * c
    return np.stack([r0, r1], axis=-1).reshape(t.shape)


def setup_inputs():
    s = mx_kscale(DIM)
    ang = np.arange(CACHE, CACHE + N)[:, None] * (1.0 / THETA ** (np.arange(0, D, 2) / D))[None, :]
    return {"x": bf(np.random.standard_normal((B, N, DIM)) * s),
            "freqs_cos": bf(np.cos(ang)), "freqs_sin": bf(np.sin(ang)),
            "Wq": bf(np.random.standard_normal((H * D, DIM)) / np.sqrt(DIM) / s[None, :]),
            "Wk": bf(np.random.standard_normal((HKV * D, DIM)) / np.sqrt(DIM) / s[None, :]),
            "Wv": bf(np.random.standard_normal((HKV * D, DIM)) / np.sqrt(DIM) / s[None, :]),
            "wq_norm": bf(2.0 + 0.2 * np.random.standard_normal(D)),
            "wk_norm": bf(1.0 + 0.1 * np.random.standard_normal(D))}


def reference(x, freqs_cos, freqs_sin, Wq, Wk, Wv, wq_norm, wk_norm):
    xq = mxq(f64(x), 2, "e5m2")
    q = (xq @ mxq(f64(Wq), 1, "e5m2").T).reshape(B, N, H, D).transpose(0, 2, 1, 3)
    k = (xq @ mxq(f64(Wk), 1, "e5m2").T).reshape(B, N, HKV, D).transpose(0, 2, 1, 3)
    v = (xq @ mxq(f64(Wv), 1, "e5m2").T).reshape(B, N, HKV, D).transpose(0, 2, 1, 3)
    q = rms_norm(q, f64(wq_norm))
    k = rms_norm(k, f64(wk_norm))
    q = rope(q, f64(freqs_cos), f64(freqs_sin))
    k = rope(k, f64(freqs_cos), f64(freqs_sin))
    return q, k, v

@@ -1,0 +1,248 @@
+from contextlib import ExitStack
+
+import concourse.mybir as mybir
+from concourse.masks import make_identity
+
+TOKENS, DIM, HEAD = 512, 2048, 128
+FEATURES = 3072
+EPS = 1e-6
+FLOPS = 2 * TOKENS * FEATURES * DIM
+
+F32 = mybir.dt.float32
+BF16 = mybir.dt.bfloat16
+U32 = mybir.dt.uint32
+U8 = mybir.dt.uint8
+E5M2X4 = mybir.dt.float8_e5m2_x4
+ACT = mybir.ActivationFunctionType
+ALU = mybir.AluOpType
+
+P = 128
+K_PASS = 512
+PASSES = DIM // K_PASS
+ROWS = 512
+TILES = ROWS // P
+PAIRS = HEAD // 2
+Q_GROUPS = 4
+K_GROUP, V_GROUP = 4, 5
+GROUPS = 6
+STEPS = PASSES + 2 * (GROUPS - 1)
+
+
+def tile_slidingcacheattention_pa_kernel(
+    tc, x, freqs_cos, freqs_sin, Wq, Wk, Wv, wq_norm, wk_norm, out_0, out_1, out_2
+):
+    nc = tc.nc
+
+    weights = [Wq[ROWS * g : ROWS * (g + 1), :] for g in range(Q_GROUPS)] + [Wk, Wv]
+    weights = [w.rearrange("(t p) k -> p t k", p=P) for w in weights]
+    results = [out_0[0, TILES * g : TILES * (g + 1)] for g in range(Q_GROUPS)] + [out_1[0], out_2[0]]
+    results = [r.rearrange("h (p j) d -> p h j d", j=TILES) for r in results]
+    x_rows = x[0].rearrange("(p j) k -> p j k", j=TILES)
+
+    with ExitStack() as ctx:
+        keep = ctx.enter_context(tc.tile_pool(name="keep", bufs=1))
+        work = ctx.enter_context(tc.tile_pool(name="work", bufs=3))
+        psum = ctx.enter_context(tc.psum_pool(name="psum", bufs=4))
+        ctx.enter_context(tc.manual_schedule())
+
+        ident = keep.tile([P, P], F32, name="ident")
+        make_identity(nc, ident[:])
+
+        gain_row = keep.tile([P, 2 * HEAD], BF16, name="gain_row")
+        ones = keep.tile([P, P], BF16, name="ones")
+        nc.vector.memset(gain_row[:], 0.0)
+        nc.vector.memset(ones[:], 1.0)
+
+        trig = keep.tile([P, 3, TILES * PAIRS], BF16, name="trig")
+        blocks = []
+        for s in range(PASSES):
+            cols = slice(K_PASS * s, K_PASS * (s + 1))
+            x_raw = keep.tile([P, TILES, K_PASS], BF16, name="x_raw%d" % s)
+            w_raw = keep.tile([P, TILES, K_PASS], BF16, name="w_raw%d" % s)
+            if s == 0:
+                nc.sync.dma_start(out=x_raw[:, 0:2, :], in_=x_rows[:, 0:2, cols])
+                nc.sync.dma_start(out=x_raw[:, 2:4, :], in_=x_rows[:, 2:4, cols])
+            else:
+                nc.sync.dma_start(out=x_raw[:], in_=x_rows[:, :, cols])
+            nc.sync.dma_start(out=w_raw[:], in_=weights[0][:, :, cols])
+            blocks.append([x_raw[:], w_raw[:]])
+            if s == 0:
+                nc.sync.dma_start(out=gain_row[0:1, 0:HEAD], in_=wq_norm.unsqueeze(0))
+                nc.sync.dma_start(out=gain_row[0:1, HEAD:], in_=wk_norm.unsqueeze(0))
+            if s == 1:
+                nc.sync.dma_start(out=trig[:, 1, :], in_=freqs_cos.rearrange("(p j) i -> p (j i)", j=TILES))
+                nc.sync.dma_start(out=trig[:, 2, :], in_=freqs_sin.rearrange("(p j) i -> p (j i)", j=TILES))
+        for s in range(PASSES, STEPS):
+            group, half = 1 + (s - PASSES) // 2, (s - PASSES) % 2
+            raw = keep.tile([P, TILES, 2 * K_PASS], BF16, name="raw%d" % s)
+            nc.sync.dma_start(out=raw[:], in_=weights[group][:, :, 2 * K_PASS * half : 2 * K_PASS * (half + 1)])
+            blocks.append([raw[:, :, 0:K_PASS], raw[:, :, K_PASS:]])
+
+        gains = keep.tile([P, 2, PAIRS, 2], F32, name="gains")
+
+        def spread_gains():
+            gain_psum = psum.tile([P, 2 * HEAD], F32, name="gain_psum", tag="turn")
+            nc.tensor.matmul(gain_psum[:], lhsT=ones[:], rhs=gain_row[:], start=True, stop=True)
+            nc.vector.tensor_copy(out=gains[:].rearrange("p a i e -> p (a i e)"), in_=gain_psum[:])
+
+        tables = keep.tile([P, 2, 2, TILES, PAIRS, 2], F32, name="tables")
+
+        def make_tables(a):
+            for e in range(2):
+                angles = trig[:, 1 - e : 3 - e, :].rearrange("p c (j i) -> p j i c", j=TILES)
+                gain = gains[:, a, :, e : e + 1].unsqueeze(1).broadcast_to([P, TILES, PAIRS, 2])
+                nc.vector.tensor_tensor(out=tables[:, a, e], in0=angles, in1=gain, op=ALU.mult)
+
+        codes, scales, staged = {}, {}, {}
+
+        def transpose_bank(s, n):
+            b, pair = divmod(n, 2)
+            bank = psum.tile([P, 2, 2, P], F32, name="bank", tag="turn")
+            for t in range(2):
+                words = blocks[s][b][:, 2 * pair + t, :].bitcast(F32)
+                for u in range(2):
+                    nc.tensor.transpose(bank[:, t, u, :], words[:, u : K_PASS // 2 : 2], ident[:])
+            return bank
+
+        def empty_bank(s, n, bank):
+            if n == 0:
+                staged[s] = work.tile([P, 2 * ROWS * 4], BF16, name="stage", align_bytes=64)
+            words = staged[s][:].bitcast(F32).rearrange("p (n t r u) -> p n t r u", n=4, t=2, u=2)
+            nc.scalar.copy(out=words[:, n], in_=bank[:].rearrange("p t u r -> p t r u"))
+
+        def quantise(s):
+            if s < PASSES:
+                codes[s] = keep.tile([P, 2 * ROWS], U32, name="codes%d" % s, align_bytes=64)
+                scales[s] = keep.tile([P, 2 * ROWS], U8, name="scales%d" % s, align_bytes=64)
+            else:
+                codes[s] = work.tile([P, 2 * ROWS], U32, name="w_codes", bufs=4, align_bytes=64)
+                scales[s] = work.tile([P, 2 * ROWS], U8, name="w_scales", bufs=4, align_bytes=64)
+            nc.vector.quantize_mx(out=codes[s][:].bitcast(E5M2X4), scales=scales[s][:], in_=staged[s][:])
+
+        acc = {}
+
+        def multiply(group, j, g):
+            if g == 0:
+                acc[group, j] = psum.tile([P, ROWS], F32, name="acc", tag="turn" if group == V_GROUP else "acc")
+            s, b = (g, 1) if group == 0 else (PASSES + 2 * (group - 1) + g // 2, g % 2)
+            tokens = slice(P * j, P * (j + 1))
+            features = slice(ROWS * b, ROWS * (b + 1))
+            nc.tensor.matmul_mx(
+                out=acc[group, j][:],
+                lhsT=codes[g][:, tokens].bitcast(E5M2X4),
+                lhsT_scale=scales[g][:, tokens],
+                rhs=codes[s][:, features].bitcast(E5M2X4),
+                rhs_scale=scales[s][:, features],
+                start=(g == 0),
+                stop=(g == PASSES - 1),
+            )
+
+        sums, roots, rstd, staged_out = {}, {}, {}, {}
+
+        def squares(group, j):
+            junk = work.tile([P, ROWS], F32, name="junk", bufs=2)
+            sums[group, j] = work.tile([P, TILES], F32, name="sums")
+            for h in range(TILES):
+                cols = slice(HEAD * h, HEAD * (h + 1))
+                nc.scalar.activation(
+                    out=junk[:, cols], in_=acc[group, j][:, cols], func=ACT.Square, accum_out=sums[group, j][:, h : h + 1]
+                )
+
+        def root(group, j):
+            roots[group, j] = work.tile([P, TILES], F32, name="roots")
+            nc.scalar.activation(out=roots[group, j][:], in_=sums[group, j][:], func=ACT.Sqrt, scale=1.0 / HEAD, bias=EPS)
+
+        def invert(group, j):
+            rstd[group, j] = work.tile([P, TILES], F32, name="rstd")
+            nc.vector.reciprocal(out=rstd[group, j][:], in_=roots[group, j][:])
+
+        def out_tile(group, j):
+            if j == 0:
+                staged_out[group] = work.tile([P, TILES, TILES, HEAD], F32, name="result")
+            return staged_out[group]
+
+        def store(group, j):
+            width = {K_GROUP: 2, V_GROUP: 1}.get(group, TILES)
+            if (j + 1) % width == 0:
+                js = slice(j + 1 - width, j + 1)
+                nc.sync.dma_start(out=results[group][:, :, js, :], in_=staged_out[group][:, :, js, :])
+
+        def rotate(group, j):
+            a = 1 if group == K_GROUP else 0
+            parts = work.tile([P, 2, TILES, PAIRS, 2], F32, name="parts")
+            t = acc[group, j][:].rearrange("p (h i e) -> p h i e", h=TILES, e=2)
+            for e in range(2):
+                for h in range(TILES):
+                    nc.vector.scalar_tensor_tensor(
+                        out=parts[:, e, h],
+                        in0=t[:, h, :, e : e + 1].broadcast_to([P, PAIRS, 2]),
+                        scalar=rstd[group, j][:, h : h + 1],
+                        in1=tables[:, a, e, j],
+                        op0=ALU.mult,
+                        op1=ALU.mult,
+                    )
+            flat = parts[:].rearrange("p e h i c -> p e h (i c)")
+            nc.gpsimd.tensor_tensor(out=out_tile(group, j)[:, :, j, :], in0=flat[:, 0], in1=flat[:, 1], op=ALU.add)
+            store(group, j)
+
+        def passes_after(s):
+            if s == 0:
+                return []
+            if s < PASSES:
+                return [(0, j, s - 1) for j in range(TILES)]
+            group, half = divmod(s - PASSES, 2)
+            first = PASSES - 1 if group == 0 else 0
+            return [(group, j, g) for j in (2 * half, 2 * half + 1) for g in range(first, PASSES)]
+
+        def finished(s, which):
+            if PASSES <= s < STEPS:
+                group, half = divmod(s - PASSES, 2)
+                return [(group, 2 * half + which)]
+            return []
+
+        def vector_epilogue(s):
+            for key in finished(s - 1, 0):
+                invert(*key)
+            for key in finished(s - 2, 1):
+                rotate(*key)
+            for key in finished(s - 1, 1):
+                invert(*key)
+            for key in finished(s - 1, 0):
+                rotate(*key)
+
+        for s in range(STEPS):
+            banks = [transpose_bank(s, n) for n in range(4)]
+            for key in finished(s - 1, 1):
+                squares(*key)
+            empty_bank(s, 0, banks[0])
+            for key in finished(s - 1, 1):
+                root(*key)
+            for n in range(1, 4):
+                empty_bank(s, n, banks[n])
+            vector_epilogue(s)
+            quantise(s)
+            if s == 2:
+                nc.vector.tensor_scalar_mul(out=trig[:, 0, :], in0=trig[:, 2, :], scalar1=-1.0)
+                make_tables(0)
+            if s == 3:
+                make_tables(1)
+            for key in passes_after(s):
+                multiply(*key)
+            if s == 1:
+                spread_gains()
+            for key in finished(s, 0):
+                squares(*key)
+                root(*key)
+
+        squares(K_GROUP, 3)
+        root(K_GROUP, 3)
+        vector_epilogue(STEPS)
+        for j in range(TILES):
+            for g in range(PASSES):
+                multiply(V_GROUP, j, g)
+            nc.scalar.copy(
+                out=out_tile(V_GROUP, j)[:, :, j, :], in_=acc[V_GROUP, j][:].rearrange("p (h d) -> p h d", h=TILES)
+            )
+            if j == 2:
+                rotate(K_GROUP, 3)
+            store(V_GROUP, j)

@@ -26,6 +26,9 @@ Q_GROUPS = 4
 K_GROUP, V_GROUP = 4, 5
 GROUPS = 6
 STEPS = PASSES + 2 * (GROUPS - 1)
+RAW_STEPS = 10
+FIRST_SORTED = 3
+STEADY_SORTED = 1
 
 
 def tile_slidingcacheattention_pa_kernel(
@@ -54,34 +57,40 @@ def tile_slidingcacheattention_pa_kernel(
         nc.vector.memset(ones[:], 1.0)
 
         trig = keep.tile([P, 3, TILES * PAIRS], BF16, name="trig")
-        blocks = []
-        for s in range(PASSES):
-            cols = slice(K_PASS * s, K_PASS * (s + 1))
-            x_raw = keep.tile([P, TILES, K_PASS], BF16, name="x_raw%d" % s)
-            w_raw = keep.tile([P, TILES, K_PASS], BF16, name="w_raw%d" % s)
-            if s == 0:
-                nc.sync.dma_start(out=x_raw[:, 0:2, :], in_=x_rows[:, 0:2, cols])
-                nc.sync.dma_start(out=x_raw[:, 2:4, :], in_=x_rows[:, 2:4, cols])
-            else:
-                nc.sync.dma_start(out=x_raw[:], in_=x_rows[:, :, cols])
-            nc.sync.dma_start(out=w_raw[:], in_=weights[0][:, :, cols])
-            blocks.append([x_raw[:], w_raw[:]])
-            if s == 0:
-                nc.sync.dma_start(out=gain_row[0:1, 0:HEAD], in_=wq_norm.unsqueeze(0))
-                nc.sync.dma_start(out=gain_row[0:1, HEAD:], in_=wk_norm.unsqueeze(0))
-            if s == 1:
-                nc.sync.dma_start(out=trig[:, 1, :], in_=freqs_cos.rearrange("(p j) i -> p (j i)", j=TILES))
-                nc.sync.dma_start(out=trig[:, 2, :], in_=freqs_sin.rearrange("(p j) i -> p (j i)", j=TILES))
-        for s in range(PASSES, STEPS):
-            group, half = 1 + (s - PASSES) // 2, (s - PASSES) % 2
-            raw = keep.tile([P, TILES, 2 * K_PASS], BF16, name="raw%d" % s)
-            nc.sync.dma_start(out=raw[:], in_=weights[group][:, :, 2 * K_PASS * half : 2 * K_PASS * (half + 1)])
-            blocks.append([raw[:, :, 0:K_PASS], raw[:, :, K_PASS:]])
+
+        def step_of(group, g):
+            if group is None:
+                return 2 * (g // 2)
+            if group == 0:
+                return 2 * (g // 2) + 1
+            return PASSES + 2 * (group - 1) + g // 2
+
+        sources = {}
+        for half in range(2):
+            cols = slice(2 * K_PASS * half, 2 * K_PASS * (half + 1))
+            sources[step_of(None, 2 * half)] = x_rows[:, :, cols]
+            for group in range(GROUPS):
+                sources[step_of(group, 2 * half)] = weights[group][:, :, cols]
+
+        raw = {}
+
+        def load(s):
+            for pair in range(2):
+                raw[s, pair] = work.tile([P, 2, 2 * K_PASS], BF16, name="raw", bufs=2 * RAW_STEPS)
+                nc.sync.dma_start(out=raw[s, pair][:], in_=sources[s][:, 2 * pair : 2 * pair + 2, :])
+
+        load(0)
+        nc.sync.dma_start(out=gain_row[0:1, 0:HEAD], in_=wq_norm.unsqueeze(0))
+        nc.sync.dma_start(out=gain_row[0:1, HEAD:], in_=wk_norm.unsqueeze(0))
+        nc.sync.dma_start(out=trig[:, 1, :], in_=freqs_cos.rearrange("(p j) i -> p (j i)", j=TILES))
+        nc.sync.dma_start(out=trig[:, 2, :], in_=freqs_sin.rearrange("(p j) i -> p (j i)", j=TILES))
+        for s in range(1, RAW_STEPS):
+            load(s)
 
         gains = keep.tile([P, 2, PAIRS, 2], F32, name="gains")
 
         def spread_gains():
-            gain_psum = psum.tile([P, 2 * HEAD], F32, name="gain_psum", tag="turn")
+            gain_psum = psum.tile([P, 2 * HEAD], F32, name="gain_psum", tag="acc")
             nc.tensor.matmul(gain_psum[:], lhsT=ones[:], rhs=gain_row[:], start=True, stop=True)
             nc.vector.tensor_copy(out=gains[:].rearrange("p a i e -> p (a i e)"), in_=gain_psum[:])
 
@@ -93,27 +102,39 @@ def tile_slidingcacheattention_pa_kernel(
                 gain = gains[:, a, :, e : e + 1].unsqueeze(1).broadcast_to([P, TILES, PAIRS, 2])
                 nc.vector.tensor_tensor(out=tables[:, a, e], in0=angles, in1=gain, op=ALU.mult)
 
-        codes, scales, staged = {}, {}, {}
+        codes, scales, staged, sorted_words = {}, {}, {}, {}
+
+        def words_of(s, pair):
+            return raw[s, pair][:].bitcast(F32).rearrange("p t (m u) -> p t u m", u=2)
+
+        def sort_words(s):
+            if FIRST_SORTED <= s < STEPS:
+                for pair in range(2 if s < 6 else 1):
+                    width = 2 * P if s < 6 else STEADY_SORTED * P
+                    sorted_words[s, pair] = work.tile([P, 2, 2, width], F32, name="sorted", bufs=4)
+                    nc.vector.tensor_copy(out=sorted_words[s, pair][:], in_=words_of(s, pair)[:, :, :, 0:width])
 
         def transpose_bank(s, n):
-            b, pair = divmod(n, 2)
+            pair, b = divmod(n, 2)
             bank = psum.tile([P, 2, 2, P], F32, name="bank", tag="turn")
+            is_sorted = (s, pair) in sorted_words and sorted_words[s, pair].shape[3] > P * b
+            words = sorted_words[s, pair][:] if is_sorted else words_of(s, pair)
             for t in range(2):
-                words = blocks[s][b][:, 2 * pair + t, :].bitcast(F32)
                 for u in range(2):
-                    nc.tensor.transpose(bank[:, t, u, :], words[:, u : K_PASS // 2 : 2], ident[:])
+                    nc.tensor.transpose(bank[:, t, u, :], words[:, t, u, P * b : P * (b + 1)], ident[:])
             return bank
 
         def empty_bank(s, n, bank):
+            pair, b = divmod(n, 2)
             if n == 0:
                 staged[s] = work.tile([P, 2 * ROWS * 4], BF16, name="stage", align_bytes=64)
-            words = staged[s][:].bitcast(F32).rearrange("p (n t r u) -> p n t r u", n=4, t=2, u=2)
-            nc.scalar.copy(out=words[:, n], in_=bank[:].rearrange("p t u r -> p t r u"))
+            words = staged[s][:].bitcast(F32).rearrange("p (b q t r u) -> p b q t r u", b=2, q=2, t=2, u=2)
+            nc.scalar.copy(out=words[:, b, pair], in_=bank[:].rearrange("p t u r -> p t r u"))
 
         def quantise(s):
-            if s < PASSES:
-                codes[s] = keep.tile([P, 2 * ROWS], U32, name="codes%d" % s, align_bytes=64)
-                scales[s] = keep.tile([P, 2 * ROWS], U8, name="scales%d" % s, align_bytes=64)
+            if s in (step_of(None, 0), step_of(None, 2)):
+                codes[s] = keep.tile([P, 2 * ROWS], U32, name="x_codes%d" % s, align_bytes=64)
+                scales[s] = keep.tile([P, 2 * ROWS], U8, name="x_scales%d" % s, align_bytes=64)
             else:
                 codes[s] = work.tile([P, 2 * ROWS], U32, name="w_codes", bufs=4, align_bytes=64)
                 scales[s] = work.tile([P, 2 * ROWS], U8, name="w_scales", bufs=4, align_bytes=64)
@@ -121,23 +142,26 @@ def tile_slidingcacheattention_pa_kernel(
 
         acc = {}
 
-        def multiply(group, j, g):
-            if g == 0:
-                acc[group, j] = psum.tile([P, ROWS], F32, name="acc", tag="turn" if group == V_GROUP else "acc")
-            s, b = (g, 1) if group == 0 else (PASSES + 2 * (group - 1) + g // 2, g % 2)
-            tokens = slice(P * j, P * (j + 1))
-            features = slice(ROWS * b, ROWS * (b + 1))
+        def multiply(group, j, g, first=0, target=None):
+            if target is None:
+                if g == 0:
+                    acc[group, j] = psum.tile([P, ROWS], F32, name="acc", tag="acc")
+                target = acc[group, j][:]
+            width = target.shape[1]
+            xs, s, b = step_of(None, g), step_of(group, g), g % 2
+            tokens = slice(ROWS * b + P * j, ROWS * b + P * (j + 1))
+            features = slice(ROWS * b + first, ROWS * b + first + width)
             nc.tensor.matmul_mx(
-                out=acc[group, j][:],
-                lhsT=codes[g][:, tokens].bitcast(E5M2X4),
-                lhsT_scale=scales[g][:, tokens],
+                out=target,
+                lhsT=codes[xs][:, tokens].bitcast(E5M2X4),
+                lhsT_scale=scales[xs][:, tokens],
                 rhs=codes[s][:, features].bitcast(E5M2X4),
                 rhs_scale=scales[s][:, features],
                 start=(g == 0),
                 stop=(g == PASSES - 1),
             )
 
-        sums, roots, rstd, staged_out = {}, {}, {}, {}
+        sums, rstd, staged_out = {}, {}, {}
 
         def squares(group, j):
             junk = work.tile([P, ROWS], F32, name="junk", bufs=2)
@@ -149,23 +173,20 @@ def tile_slidingcacheattention_pa_kernel(
                 )
 
         def root(group, j):
-            roots[group, j] = work.tile([P, TILES], F32, name="roots")
-            nc.scalar.activation(out=roots[group, j][:], in_=sums[group, j][:], func=ACT.Sqrt, scale=1.0 / HEAD, bias=EPS)
-
-        def invert(group, j):
             rstd[group, j] = work.tile([P, TILES], F32, name="rstd")
-            nc.vector.reciprocal(out=rstd[group, j][:], in_=roots[group, j][:])
+            nc.scalar.activation(
+                out=rstd[group, j][:], in_=sums[group, j][:], func=ACT.Abs_reciprocal_sqrt, scale=1.0 / HEAD, bias=EPS
+            )
 
         def out_tile(group, j):
             if j == 0:
                 staged_out[group] = work.tile([P, TILES, TILES, HEAD], F32, name="result")
             return staged_out[group]
 
-        def store(group, j):
-            width = {K_GROUP: 2, V_GROUP: 1}.get(group, TILES)
-            if (j + 1) % width == 0:
-                js = slice(j + 1 - width, j + 1)
-                nc.sync.dma_start(out=results[group][:, :, js, :], in_=staged_out[group][:, :, js, :])
+        def store(group, js, heads=slice(0, TILES)):
+            nc.sync.dma_start(out=results[group][:, heads, js, :], in_=staged_out[group][:, heads, js, :])
+
+        vector_adds = [(K_GROUP, 1), (K_GROUP, 3)]
 
         def rotate(group, j):
             a = 1 if group == K_GROUP else 0
@@ -182,16 +203,18 @@ def tile_slidingcacheattention_pa_kernel(
                         op1=ALU.mult,
                     )
             flat = parts[:].rearrange("p e h i c -> p e h (i c)")
-            nc.gpsimd.tensor_tensor(out=out_tile(group, j)[:, :, j, :], in0=flat[:, 0], in1=flat[:, 1], op=ALU.add)
-            store(group, j)
+            adder = nc.vector if (group, j) in vector_adds else nc.gpsimd
+            adder.tensor_tensor(out=out_tile(group, j)[:, :, j, :], in0=flat[:, 0], in1=flat[:, 1], op=ALU.add)
+            if j % 2 == 1:
+                store(group, slice(j - 1, j + 1))
 
         def passes_after(s):
-            if s == 0:
+            if s < 2:
                 return []
             if s < PASSES:
-                return [(0, j, s - 1) for j in range(TILES)]
+                return [(0, j, s - 2) for j in range(TILES)]
             group, half = divmod(s - PASSES, 2)
-            first = PASSES - 1 if group == 0 else 0
+            first = 2 if group == 0 else 0
             return [(group, j, g) for j in (2 * half, 2 * half + 1) for g in range(first, PASSES)]
 
         def finished(s, which):
@@ -200,15 +223,16 @@ def tile_slidingcacheattention_pa_kernel(
                 return [(group, 2 * half + which)]
             return []
 
-        def vector_epilogue(s):
+        def vector_step(s):
             for key in finished(s - 1, 0):
-                invert(*key)
-            for key in finished(s - 2, 1):
                 rotate(*key)
+            sort_words(s + 1 if s < 5 else s + 2)
             for key in finished(s - 1, 1):
-                invert(*key)
-            for key in finished(s - 1, 0):
                 rotate(*key)
+            if s < STEPS:
+                quantise(s)
+            if s == 4:
+                sort_words(6)
 
         for s in range(STEPS):
             banks = [transpose_bank(s, n) for n in range(4)]
@@ -219,30 +243,37 @@ def tile_slidingcacheattention_pa_kernel(
                 root(*key)
             for n in range(1, 4):
                 empty_bank(s, n, banks[n])
-            vector_epilogue(s)
-            quantise(s)
-            if s == 2:
+            if s + RAW_STEPS < STEPS:
+                load(s + RAW_STEPS)
+            if s == 0:
+                spread_gains()
+            vector_step(s)
+            if s == 0:
                 nc.vector.tensor_scalar_mul(out=trig[:, 0, :], in0=trig[:, 2, :], scalar1=-1.0)
-                make_tables(0)
-            if s == 3:
-                make_tables(1)
+            if s < 2:
+                make_tables(s)
             for key in passes_after(s):
                 multiply(*key)
-            if s == 1:
-                spread_gains()
             for key in finished(s, 0):
                 squares(*key)
                 root(*key)
 
         squares(K_GROUP, 3)
         root(K_GROUP, 3)
-        vector_epilogue(STEPS)
-        for j in range(TILES):
-            for g in range(PASSES):
-                multiply(V_GROUP, j, g)
-            nc.scalar.copy(
-                out=out_tile(V_GROUP, j)[:, :, j, :], in_=acc[V_GROUP, j][:].rearrange("p (h d) -> p h d", h=TILES)
-            )
-            if j == 2:
-                rotate(K_GROUP, 3)
-            store(V_GROUP, j)
+        vector_step(STEPS)
+        out_tile(V_GROUP, 0)
+        for head_pair in range(2):
+            heads = slice(2 * head_pair, 2 * head_pair + 2)
+            for tile_pair in range(2):
+                js = slice(2 * tile_pair, 2 * tile_pair + 2)
+                bank = psum.tile([P, 2, 2 * HEAD], F32, name="v_bank", tag="turn")
+                for i in range(2):
+                    for g in range(PASSES):
+                        multiply(V_GROUP, 2 * tile_pair + i, g, 2 * HEAD * head_pair, bank[:, i, :])
+                nc.scalar.copy(
+                    out=staged_out[V_GROUP][:, heads, js, :], in_=bank[:].rearrange("p j (h d) -> p h j d", d=HEAD)
+                )
+                if head_pair == 1:
+                    store(V_GROUP, js, heads)
+            if head_pair == 0:
+                store(V_GROUP, slice(0, TILES), heads)

@@ -51,6 +51,9 @@ def tile_slidingcacheattention_pa_kernel(
         ident = keep.tile([P, P], F32, name="ident")
         make_identity(nc, ident[:])
 
+        warm = keep.tile([P, 1], F32, name="warm")
+        nc.scalar.activation(out=warm[:], in_=ident[:, 0:1], func=ACT.Abs_reciprocal_sqrt, bias=1.0)
+
         gain_row = keep.tile([P, 2 * HEAD], BF16, name="gain_row")
         ones = keep.tile([P, P], BF16, name="ones")
         nc.vector.memset(gain_row[:], 0.0)

@@ -19,15 +19,16 @@ ALU = mybir.AluOpType
 P = 128
 K_PASS = 512
 PASSES = DIM // K_PASS
-ROWS = 512
-TILES = ROWS // P
+TILES = TOKENS // P
 PAIRS = HEAD // 2
-Q_GROUPS = 4
-K_GROUP, V_GROUP = 4, 5
-GROUPS = 6
-STEPS = PASSES + 2 * (GROUPS - 1)
-RAW_STEPS = 10
-FIRST_SORTED = 3
+ROWS = 2 * P
+Q_GROUPS, K_GROUPS, V_GROUPS = 8, 2, 2
+NORMED = Q_GROUPS + K_GROUPS
+GROUPS = NORMED + V_GROUPS
+STEPS = GROUPS + 2
+X_STEPS = (0, 2)
+LOADS_AHEAD = 5
+FULLY_SORTED = (3, 4)
 STEADY_SORTED = 1
 
 
@@ -36,11 +37,18 @@ def tile_slidingcacheattention_pa_kernel(
 ):
     nc = tc.nc
 
-    weights = [Wq[ROWS * g : ROWS * (g + 1), :] for g in range(Q_GROUPS)] + [Wk, Wv]
-    weights = [w.rearrange("(t p) k -> p t k", p=P) for w in weights]
-    results = [out_0[0, TILES * g : TILES * (g + 1)] for g in range(Q_GROUPS)] + [out_1[0], out_2[0]]
-    results = [r.rearrange("h (p j) d -> p h j d", j=TILES) for r in results]
+    def step_of(group):
+        return 1 if group == 0 else group + 2
+
+    sources, results = {}, []
     x_rows = x[0].rearrange("(p j) k -> p j k", j=TILES)
+    for half, s in enumerate(X_STEPS):
+        sources[s] = x_rows[:, 2 * half : 2 * half + 2, :]
+    for w, out, count in ((Wq, out_0, Q_GROUPS), (Wk, out_1, K_GROUPS), (Wv, out_2, V_GROUPS)):
+        for n in range(count):
+            sources[step_of(len(results))] = w[ROWS * n : ROWS * (n + 1), :].rearrange("(t p) k -> p t k", p=P)
+            results.append(out[0, 2 * n : 2 * n + 2].rearrange("h (p j) d -> p h j d", j=TILES))
+    normed_steps = [step_of(group) for group in range(NORMED)]
 
     with ExitStack() as ctx:
         keep = ctx.enter_context(tc.tile_pool(name="keep", bufs=1))
@@ -50,6 +58,7 @@ def tile_slidingcacheattention_pa_kernel(
 
         ident = keep.tile([P, P], F32, name="ident")
         make_identity(nc, ident[:])
+        split = keep.tile([P, 2, PAIRS], F32, name="split")
 
         warm = keep.tile([P, 1], F32, name="warm")
         nc.scalar.activation(out=warm[:], in_=ident[:, 0:1], func=ACT.Abs_reciprocal_sqrt, bias=1.0)
@@ -58,36 +67,22 @@ def tile_slidingcacheattention_pa_kernel(
         ones = keep.tile([P, P], BF16, name="ones")
         nc.vector.memset(gain_row[:], 0.0)
         nc.vector.memset(ones[:], 1.0)
+        nc.vector.tensor_copy(out=split[:], in_=ident[:].rearrange("p (i e) -> p e i", e=2))
 
         trig = keep.tile([P, 3, TILES * PAIRS], BF16, name="trig")
-
-        def step_of(group, g):
-            if group is None:
-                return 2 * (g // 2)
-            if group == 0:
-                return 2 * (g // 2) + 1
-            return PASSES + 2 * (group - 1) + g // 2
-
-        sources = {}
-        for half in range(2):
-            cols = slice(2 * K_PASS * half, 2 * K_PASS * (half + 1))
-            sources[step_of(None, 2 * half)] = x_rows[:, :, cols]
-            for group in range(GROUPS):
-                sources[step_of(group, 2 * half)] = weights[group][:, :, cols]
-
         raw = {}
 
         def load(s):
-            for pair in range(2):
-                raw[s, pair] = work.tile([P, 2, 2 * K_PASS], BF16, name="raw", bufs=2 * RAW_STEPS)
-                nc.sync.dma_start(out=raw[s, pair][:], in_=sources[s][:, 2 * pair : 2 * pair + 2, :])
+            raw[s] = work.tile([P, 2, DIM], BF16, name="raw", bufs=LOADS_AHEAD + 1)
+            for t in range(2):
+                nc.sync.dma_start(out=raw[s][:, t, :], in_=sources[s][:, t, :])
 
         load(0)
         nc.sync.dma_start(out=gain_row[0:1, 0:HEAD], in_=wq_norm.unsqueeze(0))
         nc.sync.dma_start(out=gain_row[0:1, HEAD:], in_=wk_norm.unsqueeze(0))
         nc.sync.dma_start(out=trig[:, 1, :], in_=freqs_cos.rearrange("(p j) i -> p (j i)", j=TILES))
         nc.sync.dma_start(out=trig[:, 2, :], in_=freqs_sin.rearrange("(p j) i -> p (j i)", j=TILES))
-        for s in range(1, RAW_STEPS):
+        for s in range(1, LOADS_AHEAD):
             load(s)
 
         gains = keep.tile([P, 2, PAIRS, 2], F32, name="gains")
@@ -97,186 +92,168 @@ def tile_slidingcacheattention_pa_kernel(
             nc.tensor.matmul(gain_psum[:], lhsT=ones[:], rhs=gain_row[:], start=True, stop=True)
             nc.vector.tensor_copy(out=gains[:].rearrange("p a i e -> p (a i e)"), in_=gain_psum[:])
 
-        tables = keep.tile([P, 2, 2, TILES, PAIRS, 2], F32, name="tables")
+        tables = keep.tile([P, 2, TILES, 2, PAIRS, 2], F32, name="tables")
 
         def make_tables(a):
             for e in range(2):
                 angles = trig[:, 1 - e : 3 - e, :].rearrange("p c (j i) -> p j i c", j=TILES)
                 gain = gains[:, a, :, e : e + 1].unsqueeze(1).broadcast_to([P, TILES, PAIRS, 2])
-                nc.vector.tensor_tensor(out=tables[:, a, e], in0=angles, in1=gain, op=ALU.mult)
+                nc.vector.tensor_tensor(out=tables[:, a, :, e], in0=angles, in1=gain, op=ALU.mult)
 
         codes, scales, staged, sorted_words = {}, {}, {}, {}
 
-        def words_of(s, pair):
-            return raw[s, pair][:].bitcast(F32).rearrange("p t (m u) -> p t u m", u=2)
+        def words_of(s):
+            return raw[s][:].bitcast(F32).rearrange("p t (m u) -> p t u m", u=2)
+
+        def sorted_banks(s):
+            if s < FULLY_SORTED[0] or s >= STEPS:
+                return 0
+            return 4 if s in FULLY_SORTED else STEADY_SORTED
 
         def sort_words(s):
-            if FIRST_SORTED <= s < STEPS:
-                for pair in range(2 if s < 6 else 1):
-                    width = 2 * P if s < 6 else STEADY_SORTED * P
-                    sorted_words[s, pair] = work.tile([P, 2, 2, width], F32, name="sorted", bufs=4)
-                    nc.vector.tensor_copy(out=sorted_words[s, pair][:], in_=words_of(s, pair)[:, :, :, 0:width])
+            count = sorted_banks(s)
+            if count:
+                rows, width = (2, 4 * P) if count == 4 else (1, 2 * P * count)
+                sorted_words[s] = work.tile([P, rows, 2, width], F32, name="sorted", bufs=2)
+                nc.vector.tensor_copy(out=sorted_words[s][:], in_=words_of(s)[:, 0:rows, :, 0:width])
 
         def transpose_bank(s, n):
-            pair, b = divmod(n, 2)
+            t, half = divmod(n, 2)
             bank = psum.tile([P, 2, 2, P], F32, name="bank", tag="turn")
-            is_sorted = (s, pair) in sorted_words and sorted_words[s, pair].shape[3] > P * b
-            words = sorted_words[s, pair][:] if is_sorted else words_of(s, pair)
-            for t in range(2):
+            words = (sorted_words[s][:] if n < sorted_banks(s) else words_of(s))[:, t]
+            order = split[:].rearrange("p e i -> p (e i)") if s in normed_steps else ident[:]
+            for i in range(2):
+                g = 2 * half + i
                 for u in range(2):
-                    nc.tensor.transpose(bank[:, t, u, :], words[:, t, u, P * b : P * (b + 1)], ident[:])
+                    nc.tensor.transpose(bank[:, i, u, :], words[:, u, P * g : P * (g + 1)], order)
             return bank
 
         def empty_bank(s, n, bank):
-            pair, b = divmod(n, 2)
+            t, half = divmod(n, 2)
             if n == 0:
-                staged[s] = work.tile([P, 2 * ROWS * 4], BF16, name="stage", align_bytes=64)
-            words = staged[s][:].bitcast(F32).rearrange("p (b q t r u) -> p b q t r u", b=2, q=2, t=2, u=2)
-            nc.scalar.copy(out=words[:, b, pair], in_=bank[:].rearrange("p t u r -> p t r u"))
+                staged[s] = work.tile([P, PASSES * ROWS * 4], BF16, name="stage", align_bytes=64)
+            words = staged[s][:].bitcast(F32).rearrange("p (g t r u) -> p g t r u", g=PASSES, t=2, u=2)
+            nc.scalar.copy(out=words[:, 2 * half : 2 * half + 2, t], in_=bank[:].rearrange("p g u r -> p g r u"))
 
         def quantise(s):
-            if s in (step_of(None, 0), step_of(None, 2)):
-                codes[s] = keep.tile([P, 2 * ROWS], U32, name="x_codes%d" % s, align_bytes=64)
-                scales[s] = keep.tile([P, 2 * ROWS], U8, name="x_scales%d" % s, align_bytes=64)
-            else:
-                codes[s] = work.tile([P, 2 * ROWS], U32, name="w_codes", bufs=4, align_bytes=64)
-                scales[s] = work.tile([P, 2 * ROWS], U8, name="w_scales", bufs=4, align_bytes=64)
+            pool, name = (keep, "x%d" % s) if s in X_STEPS else (work, "w")
+            codes[s] = pool.tile([P, PASSES * ROWS], U32, name=name + "_codes", align_bytes=64)
+            scales[s] = pool.tile([P, PASSES * ROWS], U8, name=name + "_scales", align_bytes=64)
             nc.vector.quantize_mx(out=codes[s][:].bitcast(E5M2X4), scales=scales[s][:], in_=staged[s][:])
 
-        acc = {}
+        acc, sums, rstd, staged_out = {}, {}, {}, {}
 
-        def multiply(group, j, g, first=0, target=None):
-            if target is None:
-                if g == 0:
-                    acc[group, j] = psum.tile([P, ROWS], F32, name="acc", tag="acc")
-                target = acc[group, j][:]
-            width = target.shape[1]
-            xs, s, b = step_of(None, g), step_of(group, g), g % 2
-            tokens = slice(ROWS * b + P * j, ROWS * b + P * (j + 1))
-            features = slice(ROWS * b + first, ROWS * b + first + width)
-            nc.tensor.matmul_mx(
-                out=target,
-                lhsT=codes[xs][:, tokens].bitcast(E5M2X4),
-                lhsT_scale=scales[xs][:, tokens],
-                rhs=codes[s][:, features].bitcast(E5M2X4),
-                rhs_scale=scales[s][:, features],
-                start=(g == 0),
-                stop=(g == PASSES - 1),
-            )
+        def multiply(group, half):
+            acc[group, half] = psum.tile([P, 2, ROWS], F32, name="acc", tag="acc")
+            xs, ws = X_STEPS[half], step_of(group)
+            for i in range(2):
+                for g in range(PASSES):
+                    tokens = slice(ROWS * g + P * i, ROWS * g + P * (i + 1))
+                    features = slice(ROWS * g, ROWS * (g + 1))
+                    nc.tensor.matmul_mx(
+                        out=acc[group, half][:, i, :],
+                        lhsT=codes[xs][:, tokens].bitcast(E5M2X4),
+                        lhsT_scale=scales[xs][:, tokens],
+                        rhs=codes[ws][:, features].bitcast(E5M2X4),
+                        rhs_scale=scales[ws][:, features],
+                        start=(g == 0),
+                        stop=(g == PASSES - 1),
+                    )
 
-        sums, rstd, staged_out = {}, {}, {}
-
-        def squares(group, j):
-            junk = work.tile([P, ROWS], F32, name="junk", bufs=2)
-            sums[group, j] = work.tile([P, TILES], F32, name="sums")
-            for h in range(TILES):
-                cols = slice(HEAD * h, HEAD * (h + 1))
+        def squares(group, half):
+            junk = work.tile([P, 4, HEAD], F32, name="junk", bufs=2)
+            sums[group, half] = work.tile([P, 4], F32, name="sums")
+            heads = acc[group, half][:].rearrange("p i (h d) -> p (i h) d", d=HEAD)
+            for n in range(4):
                 nc.scalar.activation(
-                    out=junk[:, cols], in_=acc[group, j][:, cols], func=ACT.Square, accum_out=sums[group, j][:, h : h + 1]
+                    out=junk[:, n, :], in_=heads[:, n, :], func=ACT.Square, accum_out=sums[group, half][:, n : n + 1]
                 )
 
-        def root(group, j):
-            rstd[group, j] = work.tile([P, TILES], F32, name="rstd")
+        def root(group, half):
+            rstd[group, half] = work.tile([P, 4], F32, name="rstd")
             nc.scalar.activation(
-                out=rstd[group, j][:], in_=sums[group, j][:], func=ACT.Abs_reciprocal_sqrt, scale=1.0 / HEAD, bias=EPS
+                out=rstd[group, half][:], in_=sums[group, half][:], func=ACT.Abs_reciprocal_sqrt, scale=1.0 / HEAD, bias=EPS
             )
 
-        def out_tile(group, j):
-            if j == 0:
-                staged_out[group] = work.tile([P, TILES, TILES, HEAD], F32, name="result")
-            return staged_out[group]
+        def out_rows(group, half):
+            if half == 0:
+                staged_out[group] = work.tile([P, 2, TILES, HEAD], F32, name="result", bufs=4)
+            return staged_out[group][:, :, 2 * half : 2 * half + 2, :]
 
-        def store(group, js, heads=slice(0, TILES)):
-            nc.sync.dma_start(out=results[group][:, heads, js, :], in_=staged_out[group][:, heads, js, :])
+        def store(group, js):
+            nc.sync.dma_start(out=results[group][:, :, js, :], in_=staged_out[group][:, :, js, :])
 
-        vector_adds = [(K_GROUP, 1), (K_GROUP, 3)]
-
-        def rotate(group, j):
-            a = 1 if group == K_GROUP else 0
-            parts = work.tile([P, 2, TILES, PAIRS, 2], F32, name="parts")
-            t = acc[group, j][:].rearrange("p (h i e) -> p h i e", h=TILES, e=2)
-            for e in range(2):
-                for h in range(TILES):
+        def rotate(group, half):
+            a = 0 if group < Q_GROUPS else 1
+            parts = work.tile([P, 2, 2, 2, HEAD], F32, name="parts")
+            for i in range(2):
+                for h in range(2):
                     nc.vector.scalar_tensor_tensor(
-                        out=parts[:, e, h],
-                        in0=t[:, h, :, e : e + 1].broadcast_to([P, PAIRS, 2]),
-                        scalar=rstd[group, j][:, h : h + 1],
-                        in1=tables[:, a, e, j],
+                        out=parts[:, h, i].rearrange("p e (n c) -> p (e n) c", c=2),
+                        in0=acc[group, half][:, i, HEAD * h : HEAD * (h + 1)].unsqueeze(2).broadcast_to([P, HEAD, 2]),
+                        scalar=rstd[group, half][:, 2 * i + h : 2 * i + h + 1],
+                        in1=tables[:, a, 2 * half + i].rearrange("p e n c -> p (e n) c"),
                         op0=ALU.mult,
                         op1=ALU.mult,
                     )
-            flat = parts[:].rearrange("p e h i c -> p e h (i c)")
-            adder = nc.vector if (group, j) in vector_adds else nc.gpsimd
-            adder.tensor_tensor(out=out_tile(group, j)[:, :, j, :], in0=flat[:, 0], in1=flat[:, 1], op=ALU.add)
-            if j % 2 == 1:
-                store(group, slice(j - 1, j + 1))
+            adder = nc.vector if group == 0 or (group, half) == (NORMED - 1, 1) else nc.gpsimd
+            adder.tensor_tensor(out=out_rows(group, half), in0=parts[:, :, :, 0, :], in1=parts[:, :, :, 1, :], op=ALU.add)
+            if half == 1:
+                store(group, slice(0, TILES))
 
-        def passes_after(s):
+        def copy_out(group, half):
+            nc.scalar.copy(out=out_rows(group, half), in_=acc[group, half][:].rearrange("p i (h d) -> p h i d", d=HEAD))
+
+        def products_after(s):
             if s < 2:
                 return []
-            if s < PASSES:
-                return [(0, j, s - 2) for j in range(TILES)]
-            group, half = divmod(s - PASSES, 2)
-            first = 2 if group == 0 else 0
-            return [(group, j, g) for j in (2 * half, 2 * half + 1) for g in range(first, PASSES)]
+            if s < 4:
+                return [(0, s - 2)]
+            return [(s - 3, 0), (s - 3, 1)]
 
-        def finished(s, which):
-            if PASSES <= s < STEPS:
-                group, half = divmod(s - PASSES, 2)
-                return [(group, 2 * half + which)]
-            return []
-
-        def vector_step(s):
-            for key in finished(s - 1, 0):
-                rotate(*key)
-            sort_words(s + 1 if s < 5 else s + 2)
-            for key in finished(s - 1, 1):
-                rotate(*key)
-            if s < STEPS:
-                quantise(s)
-            if s == 4:
-                sort_words(6)
+        def normed(s):
+            return [key for key in products_after(s) if key[0] < NORMED]
 
         for s in range(STEPS):
+            if s + LOADS_AHEAD < STEPS:
+                load(s + LOADS_AHEAD)
             banks = [transpose_bank(s, n) for n in range(4)]
-            for key in finished(s - 1, 1):
-                squares(*key)
-            empty_bank(s, 0, banks[0])
-            for key in finished(s - 1, 1):
-                root(*key)
-            for n in range(1, 4):
-                empty_bank(s, n, banks[n])
-            if s + RAW_STEPS < STEPS:
-                load(s + RAW_STEPS)
-            if s == 0:
-                spread_gains()
-            vector_step(s)
+            pending = normed(s - 1)
+            if len(pending) == 2:
+                squares(*pending[1])
+                empty_bank(s, 0, banks[0])
+                root(*pending[1])
+                for n in range(1, 4):
+                    empty_bank(s, n, banks[n])
+                rotate(*pending[0])
+                sort_words(s + 1)
+                rotate(*pending[1])
+                quantise(s)
+            else:
+                for n in range(4):
+                    empty_bank(s, n, banks[n])
+                if s == 0:
+                    spread_gains()
+                sort_words(s + 1)
+                quantise(s)
+                for key in pending:
+                    squares(*key)
+                    root(*key)
+                    rotate(*key)
             if s == 0:
                 nc.vector.tensor_scalar_mul(out=trig[:, 0, :], in0=trig[:, 2, :], scalar1=-1.0)
             if s < 2:
                 make_tables(s)
-            for key in passes_after(s):
+            for key in products_after(s):
                 multiply(*key)
-            for key in finished(s, 0):
-                squares(*key)
-                root(*key)
+            if len(normed(s)) == 2:
+                squares(*normed(s)[0])
+                root(*normed(s)[0])
 
-        squares(K_GROUP, 3)
-        root(K_GROUP, 3)
-        vector_step(STEPS)
-        out_tile(V_GROUP, 0)
-        for head_pair in range(2):
-            heads = slice(2 * head_pair, 2 * head_pair + 2)
-            for tile_pair in range(2):
-                js = slice(2 * tile_pair, 2 * tile_pair + 2)
-                bank = psum.tile([P, 2, 2 * HEAD], F32, name="v_bank", tag="turn")
-                for i in range(2):
-                    for g in range(PASSES):
-                        multiply(V_GROUP, 2 * tile_pair + i, g, 2 * HEAD * head_pair, bank[:, i, :])
-                nc.scalar.copy(
-                    out=staged_out[V_GROUP][:, heads, js, :], in_=bank[:].rearrange("p j (h d) -> p h j d", d=HEAD)
-                )
-                if head_pair == 1:
-                    store(V_GROUP, js, heads)
-            if head_pair == 0:
-                store(V_GROUP, slice(0, TILES), heads)
+        for half in range(2):
+            copy_out(NORMED, half)
+        store(NORMED, slice(0, TILES))
+        for half in range(2):
+            multiply(GROUPS - 1, half)
+            copy_out(GROUPS - 1, half)
+            store(GROUPS - 1, slice(2 * half, 2 * half + 2))

@@ -17,8 +17,8 @@ ACT = mybir.ActivationFunctionType
 ALU = mybir.AluOpType
 
 P = 128
-K_PASS = 512
-PASSES = DIM // K_PASS
+PACK = 4
+PASSES = DIM // (P * PACK)
 TILES = TOKENS // P
 PAIRS = HEAD // 2
 ROWS = 2 * P
@@ -27,9 +27,8 @@ NORMED = Q_GROUPS + K_GROUPS
 GROUPS = NORMED + V_GROUPS
 STEPS = GROUPS + 2
 X_STEPS = (0, 2)
+BANKS = 4
 LOADS_AHEAD = 5
-FULLY_SORTED = (3, 4)
-STEADY_SORTED = 1
 
 
 def tile_slidingcacheattention_pa_kernel(
@@ -53,7 +52,7 @@ def tile_slidingcacheattention_pa_kernel(
     with ExitStack() as ctx:
         keep = ctx.enter_context(tc.tile_pool(name="keep", bufs=1))
         work = ctx.enter_context(tc.tile_pool(name="work", bufs=3))
-        psum = ctx.enter_context(tc.psum_pool(name="psum", bufs=4))
+        psum = ctx.enter_context(tc.psum_pool(name="psum", bufs=BANKS))
         ctx.enter_context(tc.manual_schedule())
 
         ident = keep.tile([P, P], F32, name="ident")
@@ -77,71 +76,66 @@ def tile_slidingcacheattention_pa_kernel(
             for t in range(2):
                 nc.sync.dma_start(out=raw[s][:, t, :], in_=sources[s][:, t, :])
 
-        load(0)
+        after_x = X_STEPS[-1] + 1
+        for s in range(after_x):
+            load(s)
         nc.sync.dma_start(out=gain_row[0:1, 0:HEAD], in_=wq_norm.unsqueeze(0))
         nc.sync.dma_start(out=gain_row[0:1, HEAD:], in_=wk_norm.unsqueeze(0))
         nc.sync.dma_start(out=trig[:, 1, :], in_=freqs_cos.rearrange("(p j) i -> p (j i)", j=TILES))
         nc.sync.dma_start(out=trig[:, 2, :], in_=freqs_sin.rearrange("(p j) i -> p (j i)", j=TILES))
-        for s in range(1, LOADS_AHEAD):
+        for s in range(after_x, LOADS_AHEAD):
             load(s)
 
         gains = keep.tile([P, 2, PAIRS, 2], F32, name="gains")
+        tables = keep.tile([P, 2, TILES, 2, PAIRS, 2], F32, name="tables")
 
-        def spread_gains():
+        def make_tables():
             gain_psum = psum.tile([P, 2 * HEAD], F32, name="gain_psum", tag="acc")
             nc.tensor.matmul(gain_psum[:], lhsT=ones[:], rhs=gain_row[:], start=True, stop=True)
             nc.vector.tensor_copy(out=gains[:].rearrange("p a i e -> p (a i e)"), in_=gain_psum[:])
+            nc.vector.tensor_scalar_mul(out=trig[:, 0, :], in0=trig[:, 2, :], scalar1=-1.0)
+            for a in range(2):
+                for e in range(2):
+                    angles = trig[:, 1 - e : 3 - e, :].rearrange("p c (j i) -> p j i c", j=TILES)
+                    gain = gains[:, a, :, e : e + 1].unsqueeze(1).broadcast_to([P, TILES, PAIRS, 2])
+                    nc.vector.tensor_tensor(out=tables[:, a, :, e], in0=angles, in1=gain, op=ALU.mult)
 
-        tables = keep.tile([P, 2, TILES, 2, PAIRS, 2], F32, name="tables")
-
-        def make_tables(a):
-            for e in range(2):
-                angles = trig[:, 1 - e : 3 - e, :].rearrange("p c (j i) -> p j i c", j=TILES)
-                gain = gains[:, a, :, e : e + 1].unsqueeze(1).broadcast_to([P, TILES, PAIRS, 2])
-                nc.vector.tensor_tensor(out=tables[:, a, :, e], in0=angles, in1=gain, op=ALU.mult)
-
-        codes, scales, staged, sorted_words = {}, {}, {}, {}
-
-        def words_of(s):
-            return raw[s][:].bitcast(F32).rearrange("p t (m u) -> p t u m", u=2)
-
-        def sorted_banks(s):
-            if s < FULLY_SORTED[0] or s >= STEPS:
-                return 0
-            return 4 if s in FULLY_SORTED else STEADY_SORTED
-
-        def sort_words(s):
-            count = sorted_banks(s)
-            if count:
-                rows, width = (2, 4 * P) if count == 4 else (1, 2 * P * count)
-                sorted_words[s] = work.tile([P, rows, 2, width], F32, name="sorted", bufs=2)
-                nc.vector.tensor_copy(out=sorted_words[s][:], in_=words_of(s)[:, 0:rows, :, 0:width])
+        codes, scales, staged = {}, {}, {}
 
         def transpose_bank(s, n):
-            t, half = divmod(n, 2)
+            t, two_passes = divmod(n, 2)
             bank = psum.tile([P, 2, 2, P], F32, name="bank", tag="turn")
-            words = (sorted_words[s][:] if n < sorted_banks(s) else words_of(s))[:, t]
+            words = raw[s][:].bitcast(F32).rearrange("p t (m u) -> p t u m", u=2)[:, t]
             order = split[:].rearrange("p e i -> p (e i)") if s in normed_steps else ident[:]
             for i in range(2):
-                g = 2 * half + i
+                g = 2 * two_passes + i
                 for u in range(2):
                     nc.tensor.transpose(bank[:, i, u, :], words[:, u, P * g : P * (g + 1)], order)
             return bank
 
         def empty_bank(s, n, bank):
-            t, half = divmod(n, 2)
+            t, two_passes = divmod(n, 2)
             if n == 0:
-                staged[s] = work.tile([P, PASSES * ROWS * 4], BF16, name="stage", align_bytes=64)
+                staged[s] = work.tile([P, PASSES * ROWS * PACK], BF16, name="stage", align_bytes=64)
             words = staged[s][:].bitcast(F32).rearrange("p (g t r u) -> p g t r u", g=PASSES, t=2, u=2)
-            nc.scalar.copy(out=words[:, 2 * half : 2 * half + 2, t], in_=bank[:].rearrange("p g u r -> p g r u"))
+            nc.scalar.copy(
+                out=words[:, 2 * two_passes : 2 * two_passes + 2, t], in_=bank[:].rearrange("p g u r -> p g r u")
+            )
 
-        def quantise(s):
+        def quantise(s, calls):
             pool, name = (keep, "x%d" % s) if s in X_STEPS else (work, "w")
             codes[s] = pool.tile([P, PASSES * ROWS], U32, name=name + "_codes", align_bytes=64)
             scales[s] = pool.tile([P, PASSES * ROWS], U8, name=name + "_scales", align_bytes=64)
-            nc.vector.quantize_mx(out=codes[s][:].bitcast(E5M2X4), scales=scales[s][:], in_=staged[s][:])
+            width = PASSES * ROWS // calls
+            for n in range(calls):
+                cols = slice(width * n, width * (n + 1))
+                nc.vector.quantize_mx(
+                    out=codes[s][:, cols].bitcast(E5M2X4),
+                    scales=scales[s][:, cols],
+                    in_=staged[s][:, PACK * width * n : PACK * width * (n + 1)],
+                )
 
-        acc, sums, rstd, staged_out = {}, {}, {}, {}
+        acc, sums, rstd, parts, staged_out = {}, {}, {}, {}, {}
 
         def multiply(group, half):
             acc[group, half] = psum.tile([P, 2, ROWS], F32, name="acc", tag="acc")
@@ -160,16 +154,16 @@ def tile_slidingcacheattention_pa_kernel(
                         stop=(g == PASSES - 1),
                     )
 
-        def squares(group, half):
-            junk = work.tile([P, 4, HEAD], F32, name="junk", bufs=2)
+        def sum_squares(group, half):
+            squared = work.tile([P, 4, HEAD], F32, name="squared", bufs=2)
             sums[group, half] = work.tile([P, 4], F32, name="sums")
             heads = acc[group, half][:].rearrange("p i (h d) -> p (i h) d", d=HEAD)
             for n in range(4):
                 nc.scalar.activation(
-                    out=junk[:, n, :], in_=heads[:, n, :], func=ACT.Square, accum_out=sums[group, half][:, n : n + 1]
+                    out=squared[:, n, :], in_=heads[:, n, :], func=ACT.Square, accum_out=sums[group, half][:, n : n + 1]
                 )
 
-        def root(group, half):
+        def inverse_root(group, half):
             rstd[group, half] = work.tile([P, 4], F32, name="rstd")
             nc.scalar.activation(
                 out=rstd[group, half][:], in_=sums[group, half][:], func=ACT.Abs_reciprocal_sqrt, scale=1.0 / HEAD, bias=EPS
@@ -183,32 +177,42 @@ def tile_slidingcacheattention_pa_kernel(
         def store(group, js):
             nc.sync.dma_start(out=results[group][:, :, js, :], in_=staged_out[group][:, :, js, :])
 
+        def store_half(group, half):
+            store(group, slice(2 * half, 2 * half + 2))
+
         def rotate(group, half):
             a = 0 if group < Q_GROUPS else 1
-            parts = work.tile([P, 2, 2, 2, HEAD], F32, name="parts")
+            parts[group, half] = work.tile([P, 2, 2, 2, HEAD], F32, name="parts")
             for i in range(2):
                 for h in range(2):
                     nc.vector.scalar_tensor_tensor(
-                        out=parts[:, h, i].rearrange("p e (n c) -> p (e n) c", c=2),
+                        out=parts[group, half][:, h, i].rearrange("p e (n c) -> p (e n) c", c=2),
                         in0=acc[group, half][:, i, HEAD * h : HEAD * (h + 1)].unsqueeze(2).broadcast_to([P, HEAD, 2]),
                         scalar=rstd[group, half][:, 2 * i + h : 2 * i + h + 1],
                         in1=tables[:, a, 2 * half + i].rearrange("p e n c -> p (e n) c"),
                         op0=ALU.mult,
                         op1=ALU.mult,
                     )
-            adder = nc.vector if group == 0 or (group, half) == (NORMED - 1, 1) else nc.gpsimd
-            adder.tensor_tensor(out=out_rows(group, half), in0=parts[:, :, :, 0, :], in1=parts[:, :, :, 1, :], op=ALU.add)
-            if half == 1:
+
+        def add_parts(engine, group, half):
+            both = parts[group, half]
+            engine.tensor_tensor(out=out_rows(group, half), in0=both[:, :, :, 0, :], in1=both[:, :, :, 1, :], op=ALU.add)
+
+        def finish(group, half):
+            add_parts(nc.gpsimd, group, half)
+            if group == NORMED - 1:
+                store_half(group, half)
+            elif half == 1:
                 store(group, slice(0, TILES))
 
         def copy_out(group, half):
             nc.scalar.copy(out=out_rows(group, half), in_=acc[group, half][:].rearrange("p i (h d) -> p h i d", d=HEAD))
 
         def products_after(s):
-            if s < 2:
+            if s < X_STEPS[1]:
                 return []
-            if s < 4:
-                return [(0, s - 2)]
+            if s <= after_x:
+                return [(0, s - X_STEPS[1])]
             return [(s - 3, 0), (s - 3, 1)]
 
         def normed(s):
@@ -217,43 +221,45 @@ def tile_slidingcacheattention_pa_kernel(
         for s in range(STEPS):
             if s + LOADS_AHEAD < STEPS:
                 load(s + LOADS_AHEAD)
-            banks = [transpose_bank(s, n) for n in range(4)]
+            banks = [transpose_bank(s, n) for n in range(BANKS)]
             pending = normed(s - 1)
             if len(pending) == 2:
-                squares(*pending[1])
+                sum_squares(*pending[1])
                 empty_bank(s, 0, banks[0])
-                root(*pending[1])
-                for n in range(1, 4):
+                inverse_root(*pending[1])
+                for n in range(1, BANKS):
                     empty_bank(s, n, banks[n])
                 rotate(*pending[0])
-                sort_words(s + 1)
+                finish(*pending[0])
                 rotate(*pending[1])
-                quantise(s)
+                if s < STEPS - 1:
+                    finish(*pending[1])
+                    quantise(s, 1)
+                else:
+                    quantise(s, 2)
+                    add_parts(nc.vector, *pending[1])
             else:
-                for n in range(4):
+                for n in range(BANKS):
                     empty_bank(s, n, banks[n])
-                if s == 0:
-                    spread_gains()
-                sort_words(s + 1)
-                quantise(s)
+                quantise(s, 1)
                 for key in pending:
-                    squares(*key)
-                    root(*key)
+                    sum_squares(*key)
+                    inverse_root(*key)
                     rotate(*key)
-            if s == 0:
-                nc.vector.tensor_scalar_mul(out=trig[:, 0, :], in0=trig[:, 2, :], scalar1=-1.0)
-            if s < 2:
-                make_tables(s)
+                    finish(*key)
             for key in products_after(s):
                 multiply(*key)
+            if s == X_STEPS[1]:
+                make_tables()
             if len(normed(s)) == 2:
-                squares(*normed(s)[0])
-                root(*normed(s)[0])
+                sum_squares(*normed(s)[0])
+                inverse_root(*normed(s)[0])
 
         for half in range(2):
             copy_out(NORMED, half)
-        store(NORMED, slice(0, TILES))
+            store_half(NORMED, half)
+        store_half(NORMED - 1, 1)
         for half in range(2):
             multiply(GROUPS - 1, half)
             copy_out(GROUPS - 1, half)
-            store(GROUPS - 1, slice(2 * half, 2 * half + 2))
+            store_half(GROUPS - 1, half)

from contextlib import ExitStack

import concourse.mybir as mybir
from concourse.masks import make_identity

TOKENS, DIM, HEAD = 512, 2048, 128
FEATURES = 3072
EPS = 1e-6
FLOPS = 2 * TOKENS * FEATURES * DIM

F32 = mybir.dt.float32
BF16 = mybir.dt.bfloat16
U32 = mybir.dt.uint32
U8 = mybir.dt.uint8
E5M2X4 = mybir.dt.float8_e5m2_x4
ACT = mybir.ActivationFunctionType
ALU = mybir.AluOpType

P = 128
PACK = 4
PASSES = DIM // (P * PACK)
TILES = TOKENS // P
PAIRS = HEAD // 2
ROWS = 2 * P
Q_GROUPS, K_GROUPS, V_GROUPS = 8, 2, 2
NORMED = Q_GROUPS + K_GROUPS
GROUPS = NORMED + V_GROUPS
STEPS = GROUPS + 2
X_STEPS = (0, 2)
BANKS = 4
LOADS_AHEAD = 5


def tile_slidingcacheattention_pa_kernel(
    tc, x, freqs_cos, freqs_sin, Wq, Wk, Wv, wq_norm, wk_norm, out_0, out_1, out_2
):
    nc = tc.nc

    def step_of(group):
        return 1 if group == 0 else group + 2

    sources, results = {}, []
    x_rows = x[0].rearrange("(p j) k -> p j k", j=TILES)
    for half, s in enumerate(X_STEPS):
        sources[s] = x_rows[:, 2 * half : 2 * half + 2, :]
    for w, out, count in ((Wq, out_0, Q_GROUPS), (Wk, out_1, K_GROUPS), (Wv, out_2, V_GROUPS)):
        for n in range(count):
            sources[step_of(len(results))] = w[ROWS * n : ROWS * (n + 1), :].rearrange("(t p) k -> p t k", p=P)
            results.append(out[0, 2 * n : 2 * n + 2].rearrange("h (p j) d -> p h j d", j=TILES))
    normed_steps = [step_of(group) for group in range(NORMED)]

    with ExitStack() as ctx:
        keep = ctx.enter_context(tc.tile_pool(name="keep", bufs=1))
        work = ctx.enter_context(tc.tile_pool(name="work", bufs=3))
        psum = ctx.enter_context(tc.psum_pool(name="psum", bufs=BANKS))
        ctx.enter_context(tc.manual_schedule())

        ident = keep.tile([P, P], F32, name="ident")
        make_identity(nc, ident[:])
        split = keep.tile([P, 2, PAIRS], F32, name="split")

        warm = keep.tile([P, 1], F32, name="warm")
        nc.scalar.activation(out=warm[:], in_=ident[:, 0:1], func=ACT.Abs_reciprocal_sqrt, bias=1.0)

        gain_row = keep.tile([P, 2 * HEAD], BF16, name="gain_row")
        ones = keep.tile([P, P], BF16, name="ones")
        nc.vector.memset(gain_row[:], 0.0)
        nc.vector.memset(ones[:], 1.0)
        nc.vector.tensor_copy(out=split[:], in_=ident[:].rearrange("p (i e) -> p e i", e=2))

        trig = keep.tile([P, 3, TILES * PAIRS], BF16, name="trig")
        raw = {}

        def load(s):
            raw[s] = work.tile([P, 2, DIM], BF16, name="raw", bufs=LOADS_AHEAD + 1)
            for t in range(2):
                nc.sync.dma_start(out=raw[s][:, t, :], in_=sources[s][:, t, :])

        after_x = X_STEPS[-1] + 1
        for s in range(after_x):
            load(s)
        nc.sync.dma_start(out=gain_row[0:1, 0:HEAD], in_=wq_norm.unsqueeze(0))
        nc.sync.dma_start(out=gain_row[0:1, HEAD:], in_=wk_norm.unsqueeze(0))
        nc.sync.dma_start(out=trig[:, 1, :], in_=freqs_cos.rearrange("(p j) i -> p (j i)", j=TILES))
        nc.sync.dma_start(out=trig[:, 2, :], in_=freqs_sin.rearrange("(p j) i -> p (j i)", j=TILES))
        for s in range(after_x, LOADS_AHEAD):
            load(s)

        gains = keep.tile([P, 2, PAIRS, 2], F32, name="gains")
        tables = keep.tile([P, 2, TILES, 2, PAIRS, 2], F32, name="tables")

        def make_tables():
            gain_psum = psum.tile([P, 2 * HEAD], F32, name="gain_psum", tag="acc")
            nc.tensor.matmul(gain_psum[:], lhsT=ones[:], rhs=gain_row[:], start=True, stop=True)
            nc.vector.tensor_copy(out=gains[:].rearrange("p a i e -> p (a i e)"), in_=gain_psum[:])
            nc.vector.tensor_scalar_mul(out=trig[:, 0, :], in0=trig[:, 2, :], scalar1=-1.0)
            for a in range(2):
                for e in range(2):
                    angles = trig[:, 1 - e : 3 - e, :].rearrange("p c (j i) -> p j i c", j=TILES)
                    gain = gains[:, a, :, e : e + 1].unsqueeze(1).broadcast_to([P, TILES, PAIRS, 2])
                    nc.vector.tensor_tensor(out=tables[:, a, :, e], in0=angles, in1=gain, op=ALU.mult)

        codes, scales, staged = {}, {}, {}

        def transpose_bank(s, n):
            t, two_passes = divmod(n, 2)
            bank = psum.tile([P, 2, 2, P], F32, name="bank", tag="turn")
            words = raw[s][:].bitcast(F32).rearrange("p t (m u) -> p t u m", u=2)[:, t]
            order = split[:].rearrange("p e i -> p (e i)") if s in normed_steps else ident[:]
            for i in range(2):
                g = 2 * two_passes + i
                for u in range(2):
                    nc.tensor.transpose(bank[:, i, u, :], words[:, u, P * g : P * (g + 1)], order)
            return bank

        def empty_bank(s, n, bank):
            t, two_passes = divmod(n, 2)
            if n == 0:
                staged[s] = work.tile([P, PASSES * ROWS * PACK], BF16, name="stage", align_bytes=64)
            words = staged[s][:].bitcast(F32).rearrange("p (g t r u) -> p g t r u", g=PASSES, t=2, u=2)
            nc.scalar.copy(
                out=words[:, 2 * two_passes : 2 * two_passes + 2, t], in_=bank[:].rearrange("p g u r -> p g r u")
            )

        def quantise(s, calls):
            pool, name = (keep, "x%d" % s) if s in X_STEPS else (work, "w")
            codes[s] = pool.tile([P, PASSES * ROWS], U32, name=name + "_codes", align_bytes=64)
            scales[s] = pool.tile([P, PASSES * ROWS], U8, name=name + "_scales", align_bytes=64)
            width = PASSES * ROWS // calls
            for n in range(calls):
                cols = slice(width * n, width * (n + 1))
                nc.vector.quantize_mx(
                    out=codes[s][:, cols].bitcast(E5M2X4),
                    scales=scales[s][:, cols],
                    in_=staged[s][:, PACK * width * n : PACK * width * (n + 1)],
                )

        acc, sums, rstd, parts, staged_out = {}, {}, {}, {}, {}

        def multiply(group, half):
            acc[group, half] = psum.tile([P, 2, ROWS], F32, name="acc", tag="acc")
            xs, ws = X_STEPS[half], step_of(group)
            for i in range(2):
                for g in range(PASSES):
                    tokens = slice(ROWS * g + P * i, ROWS * g + P * (i + 1))
                    features = slice(ROWS * g, ROWS * (g + 1))
                    nc.tensor.matmul_mx(
                        out=acc[group, half][:, i, :],
                        lhsT=codes[xs][:, tokens].bitcast(E5M2X4),
                        lhsT_scale=scales[xs][:, tokens],
                        rhs=codes[ws][:, features].bitcast(E5M2X4),
                        rhs_scale=scales[ws][:, features],
                        start=(g == 0),
                        stop=(g == PASSES - 1),
                    )

        def sum_squares(group, half):
            squared = work.tile([P, 4, HEAD], F32, name="squared", bufs=2)
            sums[group, half] = work.tile([P, 4], F32, name="sums")
            heads = acc[group, half][:].rearrange("p i (h d) -> p (i h) d", d=HEAD)
            for n in range(4):
                nc.scalar.activation(
                    out=squared[:, n, :], in_=heads[:, n, :], func=ACT.Square, accum_out=sums[group, half][:, n : n + 1]
                )

        def inverse_root(group, half):
            rstd[group, half] = work.tile([P, 4], F32, name="rstd")
            nc.scalar.activation(
                out=rstd[group, half][:], in_=sums[group, half][:], func=ACT.Abs_reciprocal_sqrt, scale=1.0 / HEAD, bias=EPS
            )

        def out_rows(group, half):
            if half == 0:
                staged_out[group] = work.tile([P, 2, TILES, HEAD], F32, name="result", bufs=4)
            return staged_out[group][:, :, 2 * half : 2 * half + 2, :]

        def store(group, js):
            nc.sync.dma_start(out=results[group][:, :, js, :], in_=staged_out[group][:, :, js, :])

        def store_half(group, half):
            store(group, slice(2 * half, 2 * half + 2))

        def rotate(group, half):
            a = 0 if group < Q_GROUPS else 1
            parts[group, half] = work.tile([P, 2, 2, 2, HEAD], F32, name="parts")
            for i in range(2):
                for h in range(2):
                    nc.vector.scalar_tensor_tensor(
                        out=parts[group, half][:, h, i].rearrange("p e (n c) -> p (e n) c", c=2),
                        in0=acc[group, half][:, i, HEAD * h : HEAD * (h + 1)].unsqueeze(2).broadcast_to([P, HEAD, 2]),
                        scalar=rstd[group, half][:, 2 * i + h : 2 * i + h + 1],
                        in1=tables[:, a, 2 * half + i].rearrange("p e n c -> p (e n) c"),
                        op0=ALU.mult,
                        op1=ALU.mult,
                    )

        def add_parts(engine, group, half):
            both = parts[group, half]
            engine.tensor_tensor(out=out_rows(group, half), in0=both[:, :, :, 0, :], in1=both[:, :, :, 1, :], op=ALU.add)

        def finish(group, half):
            add_parts(nc.gpsimd, group, half)
            if group == NORMED - 1:
                store_half(group, half)
            elif half == 1:
                store(group, slice(0, TILES))

        def copy_out(group, half):
            nc.scalar.copy(out=out_rows(group, half), in_=acc[group, half][:].rearrange("p i (h d) -> p h i d", d=HEAD))

        def products_after(s):
            if s < X_STEPS[1]:
                return []
            if s <= after_x:
                return [(0, s - X_STEPS[1])]
            return [(s - 3, 0), (s - 3, 1)]

        def normed(s):
            return [key for key in products_after(s) if key[0] < NORMED]

        for s in range(STEPS):
            if s + LOADS_AHEAD < STEPS:
                load(s + LOADS_AHEAD)
            banks = [transpose_bank(s, n) for n in range(BANKS)]
            pending = normed(s - 1)
            if len(pending) == 2:
                sum_squares(*pending[1])
                empty_bank(s, 0, banks[0])
                inverse_root(*pending[1])
                for n in range(1, BANKS):
                    empty_bank(s, n, banks[n])
                rotate(*pending[0])
                finish(*pending[0])
                rotate(*pending[1])
                if s < STEPS - 1:
                    finish(*pending[1])
                    quantise(s, 1)
                else:
                    quantise(s, 2)
                    add_parts(nc.vector, *pending[1])
            else:
                for n in range(BANKS):
                    empty_bank(s, n, banks[n])
                quantise(s, 1)
                for key in pending:
                    sum_squares(*key)
                    inverse_root(*key)
                    rotate(*key)
                    finish(*key)
            for key in products_after(s):
                multiply(*key)
            if s == X_STEPS[1]:
                make_tables()
            if len(normed(s)) == 2:
                sum_squares(*normed(s)[0])
                inverse_root(*normed(s)[0])

        for half in range(2):
            copy_out(NORMED, half)
            store_half(NORMED, half)
        store_half(NORMED - 1, 1)
        for half in range(2):
            multiply(GROUPS - 1, half)
            copy_out(GROUPS - 1, half)
            store_half(GROUPS - 1, half)
